import numpy as np
import ml_dtypes


def mxq(x, axis, fmt="e4m3"):
    dtype, down = {"e4m3": (ml_dtypes.float8_e4m3fn, 7), "e5m2": (ml_dtypes.float8_e5m2, 14)}[fmt]
    v = np.moveaxis(np.asarray(x, np.float32).astype(ml_dtypes.bfloat16).astype(np.float64), axis, -1)
    blocks = v.reshape(v.shape[:-1] + (-1, 32))
    amax = np.abs(blocks).max(-1, keepdims=True)
    byte = np.maximum(np.where(amax > 0, np.frexp(amax)[1] - 1 + 127, 0) - down, 1)
    scale = np.exp2(byte - 127.0)
    codes = (blocks / scale).astype(np.float32).astype(dtype).astype(np.float64)
    return np.moveaxis((codes * scale).reshape(v.shape), -1, axis)


WIDE = False


def mx_kscale(k):
    if not WIDE:
        return np.ones(k)
    levels = np.array([20, -20, 10, -10, 0])
    a = np.random.permutation(np.resize(levels, k // 512 * 4)).reshape(k // 512, 4)
    idx = np.arange(k)
    return np.exp2(a[idx // 512, idx % 128 // 32])


BF16 = ml_dtypes.bfloat16


def bf(x):
    return np.asarray(x, np.float32).astype(BF16)


def f64(x):
    return np.asarray(x).astype(np.float64)


M, K, N = 1024, 2048, 1024


def softplus(v):
    return np.logaddexp(v, 0.0)


def setup_inputs():
    s = mx_kscale(M)[:, None]
    w_std0 = np.log(np.expm1(0.5 / np.sqrt(K)))
    x = np.random.standard_normal((M, K)) * s
    w_loc = np.random.standard_normal((K, N)) * 0.9 / np.sqrt(K)
    w_std = w_std0 + 0.3 * np.random.standard_normal((K, N))
    b_loc = np.random.standard_normal((1, N)) * 0.5
    b_std = -1.0 + 0.3 * np.random.standard_normal((1, N))
    eps_w = np.random.standard_normal((K, N))
    eps_b = np.random.standard_normal((1, N))
    g = np.random.standard_normal((M, N)) * np.exp2(np.random.randint(-12, 1, (M, 1))) / s
    return {"x": bf(x), "w_loc": bf(w_loc), "w_std": bf(w_std), "b_loc": bf(b_loc), "b_std": bf(b_std),
            "eps_w": bf(eps_w), "eps_b": bf(eps_b), "grad_out": bf(g)}


def reference(x, w_loc, w_std, b_loc, b_std, eps_w, eps_b, grad_out):
    return mxq(f64(x), 0, "e4m3").T @ mxq(f64(grad_out), 0, "e5m2")

@@ -1,0 +1,219 @@
+from contextlib import ExitStack
+
+import concourse.mybir as mybir
+
+BF16 = mybir.dt.bfloat16
+F32 = mybir.dt.float32
+U32 = mybir.dt.uint32
+U8 = mybir.dt.uint8
+E4M3X4 = mybir.dt.float8_e4m3fn_x4
+E5M2X4 = mybir.dt.float8_e5m2_x4
+
+P = 128
+PACK = 4
+K_PASS = P * PACK
+TOKENS, X_COLS, G_COLS = 1024, 2048, 1024
+PASSES = TOKENS // K_PASS
+N_TILE = 512
+N_HALVES = G_COLS // N_TILE
+
+FLOPS = 2 * TOKENS * X_COLS * G_COLS
+BYTES = 2 * TOKENS * (X_COLS + G_COLS) + 4 * X_COLS * G_COLS
+
+BLOCKS = ((256, 512), (256, 512, 512))
+
+
+def tile_bayesiandenselayer_kernel(
+    tc, x, w_loc, w_std, b_loc, b_std, eps_w, eps_b, grad_out, out
+):
+    nc = tc.nc
+    with ExitStack() as ctx:
+        raw = ctx.enter_context(tc.tile_pool(name="raw", bufs=1))
+        stage = ctx.enter_context(tc.tile_pool(name="stage", bufs=1))
+        packed = ctx.enter_context(tc.tile_pool(name="packed", bufs=1))
+        results = ctx.enter_context(tc.tile_pool(name="results", bufs=1))
+        psum = ctx.enter_context(tc.psum_pool(name="psum", bufs=8))
+        ctx.enter_context(tc.manual_schedule())
+
+        def load(rows, width, name):
+            t = raw.tile([P, PACK, width], BF16, name=name)
+            nc.sync.dma_start(out=t[:], in_=rows.rearrange("(p j) w -> p j w", j=PACK))
+            return t
+
+        block_width = [sum(b) for b in BLOCKS]
+        block_start = [0, block_width[0]]
+
+        def load_g(c):
+            return load(grad_out[c * K_PASS : (c + 1) * K_PASS, :], G_COLS, "g_raw%d" % c)
+
+        def load_x(c, b):
+            lo = block_start[b]
+            return load(
+                x[c * K_PASS : (c + 1) * K_PASS, lo : lo + block_width[b]],
+                block_width[b],
+                "x_raw%d_%d" % (c, b),
+            )
+
+        g_raw = {}
+        x_raw = {}
+        g_raw[0] = load_g(0)
+        x_raw[(0, 0)] = load_x(0, 0)
+        g_raw[1] = load_g(1)
+        x_raw[(1, 0)] = load_x(1, 0)
+        x_raw[(0, 1)] = load_x(0, 1)
+        x_raw[(1, 1)] = load_x(1, 1)
+
+        def make_unit(name, source, lo, width, fmt):
+            return {
+                "source": source,
+                "lo": lo,
+                "width": width,
+                "fmt": fmt,
+                "grouped": stage.tile([P, width, PACK], BF16, name=name + "_b", align_bytes=64),
+                "codes": packed.tile([P, width], U32, name=name + "_c", align_bytes=64),
+                "scales": packed.tile([P, width], U8, name=name + "_s", align_bytes=64),
+            }
+
+        g_unit = {}
+        for c in range(PASSES):
+            for h in range(N_HALVES):
+                g_unit[(c, h)] = make_unit("g%d_%d" % (c, h), g_raw[c], h * N_TILE, N_TILE, E5M2X4)
+
+        x_unit = {}
+        where = {}
+        k = 0
+        col = 0
+        for b in range(len(BLOCKS)):
+            lo = 0
+            for width in BLOCKS[b]:
+                for c in range(PASSES):
+                    x_unit[(c, k)] = make_unit("x%d_%d" % (c, k), x_raw[(c, b)], lo, width, E4M3X4)
+                for off in range(0, width, P):
+                    where[(col + off) // P] = (k, off)
+                lo += width
+                col += width
+                k += 1
+
+        def regroup(copy, u, a, b):
+            lo = u["lo"]
+            copy(
+                out=u["grouped"][:, a:b, :].rearrange("p (c i) t -> p c t i", i=4),
+                in_=u["source"][:, :, lo + a : lo + b].rearrange("p t (c i) -> p c t i", i=4),
+            )
+
+        def copy_shared(u):
+            half = u["width"] // 2
+            regroup(nc.vector.tensor_copy, u, 0, half)
+            regroup(nc.scalar.copy, u, half, u["width"])
+
+        def copy_vector(u):
+            regroup(nc.vector.tensor_copy, u, 0, u["width"])
+
+        def quantise(u):
+            nc.vector.quantize_mx(
+                out=u["codes"][:].bitcast(u["fmt"]),
+                scales=u["scales"][:],
+                in_=u["grouped"][:].rearrange("p w t -> p (w t)"),
+            )
+
+        acc = {}
+        res = {}
+
+        def mx_pass(i, c):
+            mt, h = divmod(i, N_HALVES)
+            if c == 0:
+                acc[i] = psum.tile([P, N_TILE], F32, name="acc")
+            kk, off = where[mt]
+            xu = x_unit[(c, kk)]
+            gu = g_unit[(c, h)]
+            nc.tensor.matmul_mx(
+                out=acc[i][:],
+                lhsT=xu["codes"][:, off : off + P].bitcast(E4M3X4),
+                lhsT_scale=xu["scales"][:, off : off + P],
+                rhs=gu["codes"][:].bitcast(E5M2X4),
+                rhs_scale=gu["scales"][:],
+                start=(c == 0),
+                stop=(c == PASSES - 1),
+            )
+
+        def evacuate(copy, i):
+            mt, h = divmod(i, N_HALVES)
+            if h == 0:
+                res[mt] = results.tile([P, G_COLS], F32, name="res%d" % mt)
+            copy(out=res[mt][:, h * N_TILE : (h + 1) * N_TILE], in_=acc[i][:])
+
+        def store(mt):
+            nc.sync.dma_start(out=out[mt * P : (mt + 1) * P, :], in_=res[mt][:])
+
+        def tiles_of(mts):
+            return [N_HALVES * mt + h for mt in mts for h in range(N_HALVES)]
+
+        G = g_unit
+        X = x_unit
+
+        copy_shared(G[(0, 0)])
+        copy_shared(G[(0, 1)])
+        quantise(G[(0, 0)])
+        copy_shared(X[(0, 0)])
+        quantise(G[(0, 1)])
+        copy_shared(X[(0, 1)])
+        quantise(X[(0, 0)])
+        copy_shared(G[(1, 0)])
+        quantise(X[(0, 1)])
+        for i in tiles_of([0, 1, 2, 3]):
+            mx_pass(i, 0)
+        copy_shared(G[(1, 1)])
+        quantise(G[(1, 0)])
+        copy_shared(X[(1, 0)])
+        quantise(G[(1, 1)])
+        quantise(X[(1, 0)])
+        copy_shared(X[(1, 1)])
+        for i in tiles_of([0, 1]):
+            mx_pass(i, 1)
+        evacuate(nc.scalar.copy, 0)
+        evacuate(nc.scalar.copy, 2)
+        quantise(X[(1, 1)])
+        evacuate(nc.vector.tensor_copy, 1)
+        evacuate(nc.vector.tensor_copy, 3)
+        store(0)
+        store(1)
+        for mt in (2, 3):
+            for i in tiles_of([mt]):
+                mx_pass(i, 1)
+                evacuate(nc.scalar.copy, i)
+            store(mt)
+        for mt in (4, 5):
+            for i in tiles_of([mt]):
+                mx_pass(i, 0)
+                mx_pass(i, 1)
+                evacuate(nc.scalar.copy, i)
+            store(mt)
+
+        copy_vector(X[(0, 2)])
+        copy_vector(X[(0, 3)])
+        quantise(X[(0, 2)])
+        quantise(X[(0, 3)])
+        copy_vector(X[(1, 2)])
+        for i in tiles_of([6, 7]):
+            mx_pass(i, 0)
+        copy_vector(X[(1, 3)])
+        quantise(X[(1, 2)])
+        for mt in (6, 7):
+            for i in tiles_of([mt]):
+                mx_pass(i, 1)
+                evacuate(nc.scalar.copy, i)
+            store(mt)
+        copy_vector(X[(0, 4)])
+        quantise(X[(1, 3)])
+        copy_vector(X[(1, 4)])
+        quantise(X[(0, 4)])
+        quantise(X[(1, 4)])
+        for mt in range(8, 16):
+            for i in tiles_of([mt]):
+                mx_pass(i, 0)
+                mx_pass(i, 1)
+                if i >= 21 and i % 2 == 1:
+                    evacuate(nc.vector.tensor_copy, i)
+                else:
+                    evacuate(nc.scalar.copy, i)
+            store(mt)

@@ -33,7 +33,6 @@ def tile_bayesiandenselayer_kernel(
         packed = ctx.enter_context(tc.tile_pool(name="packed", bufs=1))
         results = ctx.enter_context(tc.tile_pool(name="results", bufs=1))
         psum = ctx.enter_context(tc.psum_pool(name="psum", bufs=8))
-        ctx.enter_context(tc.manual_schedule())
 
         def load(rows, width, name):
             t = raw.tile([P, PACK, width], BF16, name=name)

@@ -33,6 +33,7 @@ def tile_bayesiandenselayer_kernel(
         packed = ctx.enter_context(tc.tile_pool(name="packed", bufs=1))
         results = ctx.enter_context(tc.tile_pool(name="results", bufs=1))
         psum = ctx.enter_context(tc.psum_pool(name="psum", bufs=8))
+        ctx.enter_context(tc.manual_schedule())
 
         def load(rows, width, name):
             t = raw.tile([P, PACK, width], BF16, name=name)
@@ -144,6 +145,11 @@ def tile_bayesiandenselayer_kernel(
         def store(mt):
             nc.sync.dma_start(out=out[mt * P : (mt + 1) * P, :], in_=res[mt][:])
 
+        def store_half(i):
+            mt, h = divmod(i, N_HALVES)
+            cols = slice(h * N_TILE, (h + 1) * N_TILE)
+            nc.sync.dma_start(out=out[mt * P : (mt + 1) * P, cols], in_=res[mt][:, cols])
+
         def tiles_of(mts):
             return [N_HALVES * mt + h for mt in mts for h in range(N_HALVES)]
 
@@ -170,11 +176,12 @@ def tile_bayesiandenselayer_kernel(
         for i in tiles_of([0, 1]):
             mx_pass(i, 1)
         evacuate(nc.scalar.copy, 0)
+        store_half(0)
         evacuate(nc.scalar.copy, 2)
         quantise(X[(1, 1)])
         evacuate(nc.vector.tensor_copy, 1)
+        store_half(1)
         evacuate(nc.vector.tensor_copy, 3)
-        store(0)
         store(1)
         for mt in (2, 3):
             for i in tiles_of([mt]):
@@ -191,17 +198,17 @@ def tile_bayesiandenselayer_kernel(
         copy_vector(X[(0, 2)])
         copy_vector(X[(0, 3)])
         quantise(X[(0, 2)])
-        quantise(X[(0, 3)])
         copy_vector(X[(1, 2)])
+        quantise(X[(0, 3)])
         for i in tiles_of([6, 7]):
             mx_pass(i, 0)
-        copy_vector(X[(1, 3)])
         quantise(X[(1, 2)])
         for mt in (6, 7):
             for i in tiles_of([mt]):
                 mx_pass(i, 1)
                 evacuate(nc.scalar.copy, i)
             store(mt)
+        copy_vector(X[(1, 3)])
         copy_vector(X[(0, 4)])
         quantise(X[(1, 3)])
         copy_vector(X[(1, 4)])
@@ -215,4 +222,7 @@ def tile_bayesiandenselayer_kernel(
                     evacuate(nc.vector.tensor_copy, i)
                 else:
                     evacuate(nc.scalar.copy, i)
-            store(mt)
+                if mt == 15:
+                    store_half(i)
+            if mt < 15:
+                store(mt)

@@ -209,8 +209,8 @@ def tile_bayesiandenselayer_kernel(
                 evacuate(nc.scalar.copy, i)
             store(mt)
         copy_vector(X[(1, 3)])
-        copy_vector(X[(0, 4)])
         quantise(X[(1, 3)])
+        copy_vector(X[(0, 4)])
         copy_vector(X[(1, 4)])
         quantise(X[(0, 4)])
         quantise(X[(1, 4)])

from contextlib import ExitStack

import concourse.mybir as mybir

BF16 = mybir.dt.bfloat16
F32 = mybir.dt.float32
U32 = mybir.dt.uint32
U8 = mybir.dt.uint8
E4M3X4 = mybir.dt.float8_e4m3fn_x4
E5M2X4 = mybir.dt.float8_e5m2_x4

P = 128
PACK = 4
K_PASS = P * PACK
TOKENS, X_COLS, G_COLS = 1024, 2048, 1024
PASSES = TOKENS // K_PASS
N_TILE = 512
N_HALVES = G_COLS // N_TILE

FLOPS = 2 * TOKENS * X_COLS * G_COLS
BYTES = 2 * TOKENS * (X_COLS + G_COLS) + 4 * X_COLS * G_COLS

BLOCKS = ((256, 512), (256, 512, 512))


def tile_bayesiandenselayer_kernel(
    tc, x, w_loc, w_std, b_loc, b_std, eps_w, eps_b, grad_out, out
):
    nc = tc.nc
    with ExitStack() as ctx:
        raw = ctx.enter_context(tc.tile_pool(name="raw", bufs=1))
        stage = ctx.enter_context(tc.tile_pool(name="stage", bufs=1))
        packed = ctx.enter_context(tc.tile_pool(name="packed", bufs=1))
        results = ctx.enter_context(tc.tile_pool(name="results", bufs=1))
        psum = ctx.enter_context(tc.psum_pool(name="psum", bufs=8))
        ctx.enter_context(tc.manual_schedule())

        def load(rows, width, name):
            t = raw.tile([P, PACK, width], BF16, name=name)
            nc.sync.dma_start(out=t[:], in_=rows.rearrange("(p j) w -> p j w", j=PACK))
            return t

        block_width = [sum(b) for b in BLOCKS]
        block_start = [0, block_width[0]]

        def load_g(c):
            return load(grad_out[c * K_PASS : (c + 1) * K_PASS, :], G_COLS, "g_raw%d" % c)

        def load_x(c, b):
            lo = block_start[b]
            return load(
                x[c * K_PASS : (c + 1) * K_PASS, lo : lo + block_width[b]],
                block_width[b],
                "x_raw%d_%d" % (c, b),
            )

        g_raw = {}
        x_raw = {}
        g_raw[0] = load_g(0)
        x_raw[(0, 0)] = load_x(0, 0)
        g_raw[1] = load_g(1)
        x_raw[(1, 0)] = load_x(1, 0)
        x_raw[(0, 1)] = load_x(0, 1)
        x_raw[(1, 1)] = load_x(1, 1)

        def make_unit(name, source, lo, width, fmt):
            return {
                "source": source,
                "lo": lo,
                "width": width,
                "fmt": fmt,
                "grouped": stage.tile([P, width, PACK], BF16, name=name + "_b", align_bytes=64),
                "codes": packed.tile([P, width], U32, name=name + "_c", align_bytes=64),
                "scales": packed.tile([P, width], U8, name=name + "_s", align_bytes=64),
            }

        g_unit = {}
        for c in range(PASSES):
            for h in range(N_HALVES):
                g_unit[(c, h)] = make_unit("g%d_%d" % (c, h), g_raw[c], h * N_TILE, N_TILE, E5M2X4)

        x_unit = {}
        where = {}
        k = 0
        col = 0
        for b in range(len(BLOCKS)):
            lo = 0
            for width in BLOCKS[b]:
                for c in range(PASSES):
                    x_unit[(c, k)] = make_unit("x%d_%d" % (c, k), x_raw[(c, b)], lo, width, E4M3X4)
                for off in range(0, width, P):
                    where[(col + off) // P] = (k, off)
                lo += width
                col += width
                k += 1

        def regroup(copy, u, a, b):
            lo = u["lo"]
            copy(
                out=u["grouped"][:, a:b, :].rearrange("p (c i) t -> p c t i", i=4),
                in_=u["source"][:, :, lo + a : lo + b].rearrange("p t (c i) -> p c t i", i=4),
            )

        def copy_shared(u):
            half = u["width"] // 2
            regroup(nc.vector.tensor_copy, u, 0, half)
            regroup(nc.scalar.copy, u, half, u["width"])

        def copy_vector(u):
            regroup(nc.vector.tensor_copy, u, 0, u["width"])

        def quantise(u):
            nc.vector.quantize_mx(
                out=u["codes"][:].bitcast(u["fmt"]),
                scales=u["scales"][:],
                in_=u["grouped"][:].rearrange("p w t -> p (w t)"),
            )

        acc = {}
        res = {}

        def mx_pass(i, c):
            mt, h = divmod(i, N_HALVES)
            if c == 0:
                acc[i] = psum.tile([P, N_TILE], F32, name="acc")
            kk, off = where[mt]
            xu = x_unit[(c, kk)]
            gu = g_unit[(c, h)]
            nc.tensor.matmul_mx(
                out=acc[i][:],
                lhsT=xu["codes"][:, off : off + P].bitcast(E4M3X4),
                lhsT_scale=xu["scales"][:, off : off + P],
                rhs=gu["codes"][:].bitcast(E5M2X4),
                rhs_scale=gu["scales"][:],
                start=(c == 0),
                stop=(c == PASSES - 1),
            )

        def evacuate(copy, i):
            mt, h = divmod(i, N_HALVES)
            if h == 0:
                res[mt] = results.tile([P, G_COLS], F32, name="res%d" % mt)
            copy(out=res[mt][:, h * N_TILE : (h + 1) * N_TILE], in_=acc[i][:])

        def store(mt):
            nc.sync.dma_start(out=out[mt * P : (mt + 1) * P, :], in_=res[mt][:])

        def store_half(i):
            mt, h = divmod(i, N_HALVES)
            cols = slice(h * N_TILE, (h + 1) * N_TILE)
            nc.sync.dma_start(out=out[mt * P : (mt + 1) * P, cols], in_=res[mt][:, cols])

        def tiles_of(mts):
            return [N_HALVES * mt + h for mt in mts for h in range(N_HALVES)]

        G = g_unit
        X = x_unit

        copy_shared(G[(0, 0)])
        copy_shared(G[(0, 1)])
        quantise(G[(0, 0)])
        copy_shared(X[(0, 0)])
        quantise(G[(0, 1)])
        copy_shared(X[(0, 1)])
        quantise(X[(0, 0)])
        copy_shared(G[(1, 0)])
        quantise(X[(0, 1)])
        for i in tiles_of([0, 1, 2, 3]):
            mx_pass(i, 0)
        copy_shared(G[(1, 1)])
        quantise(G[(1, 0)])
        copy_shared(X[(1, 0)])
        quantise(G[(1, 1)])
        quantise(X[(1, 0)])
        copy_shared(X[(1, 1)])
        for i in tiles_of([0, 1]):
            mx_pass(i, 1)
        evacuate(nc.scalar.copy, 0)
        store_half(0)
        evacuate(nc.scalar.copy, 2)
        quantise(X[(1, 1)])
        evacuate(nc.vector.tensor_copy, 1)
        store_half(1)
        evacuate(nc.vector.tensor_copy, 3)
        store(1)
        for mt in (2, 3):
            for i in tiles_of([mt]):
                mx_pass(i, 1)
                evacuate(nc.scalar.copy, i)
            store(mt)
        for mt in (4, 5):
            for i in tiles_of([mt]):
                mx_pass(i, 0)
                mx_pass(i, 1)
                evacuate(nc.scalar.copy, i)
            store(mt)

        copy_vector(X[(0, 2)])
        copy_vector(X[(0, 3)])
        quantise(X[(0, 2)])
        copy_vector(X[(1, 2)])
        quantise(X[(0, 3)])
        for i in tiles_of([6, 7]):
            mx_pass(i, 0)
        quantise(X[(1, 2)])
        for mt in (6, 7):
            for i in tiles_of([mt]):
                mx_pass(i, 1)
                evacuate(nc.scalar.copy, i)
            store(mt)
        copy_vector(X[(1, 3)])
        quantise(X[(1, 3)])
        copy_vector(X[(0, 4)])
        copy_vector(X[(1, 4)])
        quantise(X[(0, 4)])
        quantise(X[(1, 4)])
        for mt in range(8, 16):
            for i in tiles_of([mt]):
                mx_pass(i, 0)
                mx_pass(i, 1)
                if i >= 21 and i % 2 == 1:
                    evacuate(nc.vector.tensor_copy, i)
                else:
                    evacuate(nc.scalar.copy, i)
                if mt == 15:
                    store_half(i)
            if mt < 15:
                store(mt)
